import numpy as np
import ml_dtypes


def mxq(x, axis, fmt="e4m3"):
    dtype, down = {"e4m3": (ml_dtypes.float8_e4m3fn, 7), "e5m2": (ml_dtypes.float8_e5m2, 14)}[fmt]
    v = np.moveaxis(np.asarray(x, np.float32).astype(ml_dtypes.bfloat16).astype(np.float64), axis, -1)
    blocks = v.reshape(v.shape[:-1] + (-1, 32))
    amax = np.abs(blocks).max(-1, keepdims=True)
    byte = np.maximum(np.where(amax > 0, np.frexp(amax)[1] - 1 + 127, 0) - down, 1)
    scale = np.exp2(byte - 127.0)
    codes = (blocks / scale).astype(np.float32).astype(dtype).astype(np.float64)
    return np.moveaxis((codes * scale).reshape(v.shape), -1, axis)


WIDE = False


def mx_kscale(k):
    if not WIDE:
        return np.ones(k)
    levels = np.array([10, -10, 5, -5, 0])
    a = np.random.permutation(np.resize(levels, k // 512 * 4)).reshape(k // 512, 4)
    idx = np.arange(k)
    return np.exp2(a[idx // 512, idx % 128 // 32])


BF16 = ml_dtypes.bfloat16


def bf(x):
    return np.asarray(x, np.float32).astype(BF16)


def f64(x):
    return np.asarray(x).astype(np.float64)


B, Q, K, D = 8, 1024, 512, 256
C = D + D


def setup_inputs():
    s, t = mx_kscale(K), mx_kscale(C)
    z = np.exp(2.0 * np.random.standard_normal((B, Q, K)))
    return {"attn_weights": bf(z / z.sum(-1, keepdims=True) * s),
            "context": bf(np.random.standard_normal((B, K, D)) * 0.5 / s[:, None] * t[:D]),
            "q": bf(np.random.standard_normal((B, Q, D)) * 4.0 / np.sqrt(D) * t[D:]),
            "W_out": bf(np.random.standard_normal((D, C)) * 6.0 / np.sqrt(C) / t),
            "b_out": bf(np.random.standard_normal(D) * 0.2)}


def reference(attn_weights, context, q, W_out, b_out):
    mix = mxq(f64(attn_weights), 2, "e4m3") @ mxq(f64(context), 1, "e4m3")
    combined = np.concatenate([mix, f64(q)], axis=-1)
    return np.tanh((mxq(combined, 2, "e4m3") @ mxq(f64(W_out), 1, "e4m3").T) + f64(b_out))

@@ -1,0 +1,251 @@
+from contextlib import ExitStack
+
+import concourse.mybir as mybir
+from concourse.masks import make_identity
+
+BF16 = mybir.dt.bfloat16
+F32 = mybir.dt.float32
+U32 = mybir.dt.uint32
+U8 = mybir.dt.uint8
+FP8X4 = mybir.dt.float8_e4m3fn_x4
+TANH = mybir.ActivationFunctionType.Tanh
+ADD = mybir.AluOpType.add
+
+B, Q, K, D = 8, 1024, 512, 256
+C = D + D
+FLOPS = 2 * B * Q * K * D + 2 * B * Q * C * D
+
+P = 128
+PACK = 4
+ROWS_PER_PARTITION = Q // P
+UNIT_TILES = 4
+UNIT_ROWS = UNIT_TILES * P
+UNITS_PER_BATCH = Q // UNIT_ROWS
+UNITS = B * UNITS_PER_BATCH
+BANK_TILES = 2
+BANK_ROWS = BANK_TILES * P
+UNIT_BANKS = UNIT_TILES // BANK_TILES
+
+LAG_QUANTISE_A = 1
+LAG_MIX = 2
+LAG_QUANTISE_COMB = 3
+LAG_OUT = 4
+
+
+def tile_attention_pb_t_kernel(tc, attn_weights, context, q, W_out, b_out, out):
+    nc = tc.nc
+    with ExitStack() as stack:
+        stack.enter_context(tc.manual_schedule())
+        const = stack.enter_context(tc.tile_pool(name="const", bufs=1))
+        loads = stack.enter_context(tc.tile_pool(name="loads", bufs=1))
+        work = stack.enter_context(tc.tile_pool(name="work", bufs=3))
+        psum = stack.enter_context(tc.psum_pool(name="psum", bufs=2))
+
+        w_raw = const.tile([P, D // P, C], BF16)
+        nc.scalar.dma_start(out=w_raw[:], in_=W_out.rearrange("(j p) c -> p j c", p=P))
+        bias_bf16 = const.tile([P, D], BF16)
+        nc.scalar.dma_start(out=bias_bf16[:], in_=b_out.partition_broadcast(P))
+
+        a_raws, q_raws, ctx_raws = [], [], []
+        for unit in range(UNITS):
+            batch, half = divmod(unit, UNITS_PER_BATCH)
+            tiles = slice(half * UNIT_TILES, (half + 1) * UNIT_TILES)
+            a_raw = loads.tile([P, UNIT_TILES, K], BF16, tag="a_raw", bufs=UNITS)
+            nc.sync.dma_start(
+                out=a_raw[:],
+                in_=attn_weights[batch].rearrange("(p t) k -> p t k", t=ROWS_PER_PARTITION)[:, tiles, :],
+            )
+            a_raws.append(a_raw)
+            q_raw = loads.tile([P, UNIT_TILES, D], BF16, tag="q_raw", bufs=UNITS)
+            nc.sync.dma_start(
+                out=q_raw[:],
+                in_=q[batch].rearrange("(p t) d -> p t d", t=ROWS_PER_PARTITION)[:, tiles, :],
+            )
+            q_raws.append(q_raw)
+            if half == 0:
+                ctx_raw = loads.tile([P, PACK, D], BF16, tag="ctx_raw", bufs=B)
+                nc.sync.dma_start(
+                    out=ctx_raw[:].rearrange("p (u e) d -> p u (e d)", u=2),
+                    in_=context[batch].rearrange("(u p e) d -> p u (e d)", u=2, e=2),
+                )
+                ctx_raws.append(ctx_raw)
+
+        warm = const.tile([P, 1], F32)
+        nc.vector.memset(warm[:], 0.0)
+        nc.scalar.activation(out=warm[:], in_=warm[:], func=TANH)
+
+        ident = const.tile([P, P], F32)
+        make_identity(nc, ident[:])
+
+        w_words = w_raw[:].bitcast(F32)
+        w_t = psum.tile([P, 2, D], F32, tag="a_t")
+        for j in range(D // P):
+            for u in range(2):
+                nc.tensor.transpose(w_t[:, u, j * P : (j + 1) * P], w_words[:, j, u * P : (u + 1) * P], ident[:])
+        w_grouped = const.tile([P, D, PACK], BF16, align_bytes=64)
+        nc.vector.tensor_copy(out=w_grouped[:].bitcast(F32), in_=w_t[:].rearrange("p u o -> p o u"))
+        bias = const.tile([P, D], F32)
+        nc.vector.tensor_copy(out=bias[:], in_=bias_bf16[:])
+        w_codes = const.tile([P, D], U32, align_bytes=64)
+        w_scales = const.tile([P, D], U8, align_bytes=64)
+        nc.vector.quantize_mx(
+            out=w_codes[:].bitcast(FP8X4), scales=w_scales[:], in_=w_grouped[:].rearrange("p o t -> p (o t)")
+        )
+
+        a_t, q_t, a_grouped, a_codes, a_scales = {}, {}, {}, {}, {}
+        ctx_grouped, ctx_codes, ctx_scales = {}, {}, {}
+        mix_t, comb, comb_codes, comb_scales = {}, {}, {}, {}
+        out_acc, result = {}, {}
+
+        def transpose_unit(unit):
+            a_words = a_raws[unit][:].bitcast(F32)
+            q_words = q_raws[unit][:].bitcast(F32)
+            for bank in range(UNIT_BANKS):
+                words_t = psum.tile([P, 2, BANK_ROWS], F32, tag="a_t")
+                for i in range(BANK_TILES):
+                    for u in range(2):
+                        nc.tensor.transpose(
+                            words_t[:, u, i * P : (i + 1) * P],
+                            a_words[:, bank * BANK_TILES + i, u * P : (u + 1) * P],
+                            ident[:],
+                        )
+                a_t[unit, bank] = words_t
+            q_words_t = psum.tile([P, UNIT_ROWS], F32, tag="q_t")
+            for j in range(UNIT_TILES):
+                nc.tensor.transpose(q_words_t[:, j * P : (j + 1) * P], q_words[:, j, :], ident[:])
+            q_t[unit] = q_words_t
+
+        def copy_a_out(unit):
+            grouped = work.tile([P, UNIT_ROWS, PACK], BF16, tag="a_grouped", align_bytes=64)
+            for bank in range(UNIT_BANKS):
+                nc.scalar.copy(
+                    out=grouped[:, bank * BANK_ROWS : (bank + 1) * BANK_ROWS, :].bitcast(F32),
+                    in_=a_t[unit, bank][:].rearrange("p u r -> p r u"),
+                )
+            a_grouped[unit] = grouped
+
+        def copy_q_out(unit):
+            both = work.tile([P, UNIT_ROWS, PACK], BF16, tag="comb", bufs=5, align_bytes=64)
+            nc.vector.tensor_copy(
+                out=both[:].bitcast(F32),
+                in_=q_t[unit][:].unsqueeze(2).to_broadcast([P, UNIT_ROWS, 2]),
+            )
+            comb[unit] = both
+
+        def regroup_context(batch):
+            grouped = work.tile([P, 2, P, PACK], BF16, tag="ctx_grouped", bufs=2, align_bytes=64)
+            nc.vector.tensor_copy(out=grouped[:], in_=ctx_raws[batch][:].rearrange("p t (m f) -> p f m t", f=2))
+            ctx_grouped[batch] = grouped
+
+        def quantise_context(batch):
+            codes = work.tile([P, D], U32, tag="ctx_codes", align_bytes=64)
+            scales = work.tile([P, D], U8, tag="ctx_scales", align_bytes=64)
+            nc.vector.quantize_mx(
+                out=codes[:].bitcast(FP8X4),
+                scales=scales[:],
+                in_=ctx_grouped[batch][:].rearrange("p f m t -> p (f m t)"),
+            )
+            ctx_codes[batch], ctx_scales[batch] = codes, scales
+
+        def quantise_a(unit):
+            codes = work.tile([P, UNIT_ROWS], U32, tag="a_codes", align_bytes=64)
+            scales = work.tile([P, UNIT_ROWS], U8, tag="a_scales", align_bytes=64)
+            nc.vector.quantize_mx(
+                out=codes[:].bitcast(FP8X4),
+                scales=scales[:],
+                in_=a_grouped[unit][:].rearrange("p r t -> p (r t)"),
+            )
+            a_codes[unit], a_scales[unit] = codes, scales
+
+        def multiply_mix(unit):
+            batch = unit // UNITS_PER_BATCH
+            for bank in range(UNIT_BANKS):
+                rows = slice(bank * BANK_ROWS, (bank + 1) * BANK_ROWS)
+                acc = psum.tile([P, 2, BANK_ROWS], F32, tag="mix_t")
+                for f in range(2):
+                    feats = slice(f * P, (f + 1) * P)
+                    nc.tensor.matmul_mx(
+                        out=acc[:, f, :],
+                        lhsT=ctx_codes[batch][:, feats].bitcast(FP8X4),
+                        lhsT_scale=ctx_scales[batch][:, feats],
+                        rhs=a_codes[unit][:, rows].bitcast(FP8X4),
+                        rhs_scale=a_scales[unit][:, rows],
+                        start=True,
+                        stop=True,
+                    )
+                mix_t[unit, bank] = acc
+
+        def copy_mix_out(unit):
+            for bank in range(UNIT_BANKS):
+                nc.scalar.copy(
+                    out=comb[unit][:, bank * BANK_ROWS : (bank + 1) * BANK_ROWS, 0:2],
+                    in_=mix_t[unit, bank][:].rearrange("p f r -> p r f"),
+                )
+
+        def quantise_comb(unit):
+            codes = work.tile([P, UNIT_ROWS], U32, tag="comb_codes", align_bytes=64)
+            scales = work.tile([P, UNIT_ROWS], U8, tag="comb_scales", align_bytes=64)
+            nc.vector.quantize_mx(
+                out=codes[:].bitcast(FP8X4),
+                scales=scales[:],
+                in_=comb[unit][:].rearrange("p r t -> p (r t)"),
+            )
+            comb_codes[unit], comb_scales[unit] = codes, scales
+
+        def multiply_out(unit):
+            for bank in range(UNIT_BANKS):
+                acc = psum.tile([P, BANK_TILES, D], F32, tag="out_acc")
+                for i in range(BANK_TILES):
+                    j = bank * BANK_TILES + i
+                    nc.tensor.matmul_mx(
+                        out=acc[:, i, :],
+                        lhsT=comb_codes[unit][:, j * P : (j + 1) * P].bitcast(FP8X4),
+                        lhsT_scale=comb_scales[unit][:, j * P : (j + 1) * P],
+                        rhs=w_codes[:].bitcast(FP8X4),
+                        rhs_scale=w_scales[:],
+                        start=True,
+                        stop=True,
+                    )
+                out_acc[unit, bank] = acc
+
+        def add_bias(unit):
+            summed = work.tile([P, UNIT_TILES, D], F32, tag="result", bufs=6)
+            for bank in range(UNIT_BANKS):
+                nc.vector.tensor_tensor(
+                    out=summed[:, bank * BANK_TILES : (bank + 1) * BANK_TILES, :],
+                    in0=out_acc[unit, bank][:],
+                    in1=bias[:].unsqueeze(1).to_broadcast([P, BANK_TILES, D]),
+                    op=ADD,
+                )
+            result[unit] = summed
+
+        def tanh_and_store(unit):
+            batch, half = divmod(unit, UNITS_PER_BATCH)
+            tiles = slice(half * UNIT_TILES, (half + 1) * UNIT_TILES)
+            nc.scalar.activation(out=result[unit][:], in_=result[unit][:], func=TANH)
+            nc.sync.dma_start(
+                out=out[batch].rearrange("(p t) o -> p t o", t=ROWS_PER_PARTITION)[:, tiles, :],
+                in_=result[unit][:],
+            )
+
+        def run(stage, unit):
+            if 0 <= unit < UNITS:
+                stage(unit)
+
+        def run_for_batch(stage, step):
+            if step % UNITS_PER_BATCH == 0 and step < UNITS:
+                stage(step // UNITS_PER_BATCH)
+
+        for step in range(UNITS + LAG_OUT):
+            run(transpose_unit, step)
+            run(multiply_mix, step - LAG_MIX)
+            run(multiply_out, step - LAG_OUT)
+            run(copy_a_out, step)
+            run(copy_q_out, step)
+            run(add_bias, step - LAG_OUT)
+            run_for_batch(regroup_context, step)
+            run(quantise_a, step - LAG_QUANTISE_A)
+            run(copy_mix_out, step - LAG_MIX)
+            run(quantise_comb, step - LAG_QUANTISE_COMB)
+            run_for_batch(quantise_context, step)
+            run(tanh_and_store, step - LAG_OUT)

@@ -17,19 +17,20 @@ FLOPS = 2 * B * Q * K * D + 2 * B * Q * C * D
 
 P = 128
 PACK = 4
-ROWS_PER_PARTITION = Q // P
-UNIT_TILES = 4
+BATCH_TILES = Q // P
+UNIT_TILES = 2
 UNIT_ROWS = UNIT_TILES * P
-UNITS_PER_BATCH = Q // UNIT_ROWS
+UNITS_PER_BATCH = BATCH_TILES // UNIT_TILES
 UNITS = B * UNITS_PER_BATCH
-BANK_TILES = 2
-BANK_ROWS = BANK_TILES * P
-UNIT_BANKS = UNIT_TILES // BANK_TILES
+LOAD_UNITS = 2
+LOAD_TILES = LOAD_UNITS * UNIT_TILES
+LOADS_PER_BATCH = BATCH_TILES // LOAD_TILES
 
 LAG_QUANTISE_A = 1
-LAG_MIX = 2
-LAG_QUANTISE_COMB = 3
-LAG_OUT = 4
+LAG_MIX = 3
+LAG_QUANTISE_COMB = 4
+LAG_OUT = 6
+LAG_TANH = 7
 
 
 def tile_attention_pb_t_kernel(tc, attn_weights, context, q, W_out, b_out, out):
@@ -38,7 +39,7 @@ def tile_attention_pb_t_kernel(tc, attn_weights, context, q, W_out, b_out, out):
         stack.enter_context(tc.manual_schedule())
         const = stack.enter_context(tc.tile_pool(name="const", bufs=1))
         loads = stack.enter_context(tc.tile_pool(name="loads", bufs=1))
-        work = stack.enter_context(tc.tile_pool(name="work", bufs=3))
+        work = stack.enter_context(tc.tile_pool(name="work", bufs=4))
         psum = stack.enter_context(tc.psum_pool(name="psum", bufs=2))
 
         w_raw = const.tile([P, D // P, C], BF16)
@@ -47,28 +48,28 @@ def tile_attention_pb_t_kernel(tc, attn_weights, context, q, W_out, b_out, out):
         nc.scalar.dma_start(out=bias_bf16[:], in_=b_out.partition_broadcast(P))
 
         a_raws, q_raws, ctx_raws = [], [], []
-        for unit in range(UNITS):
-            batch, half = divmod(unit, UNITS_PER_BATCH)
-            tiles = slice(half * UNIT_TILES, (half + 1) * UNIT_TILES)
-            a_raw = loads.tile([P, UNIT_TILES, K], BF16, tag="a_raw", bufs=UNITS)
-            nc.sync.dma_start(
-                out=a_raw[:],
-                in_=attn_weights[batch].rearrange("(p t) k -> p t k", t=ROWS_PER_PARTITION)[:, tiles, :],
-            )
-            a_raws.append(a_raw)
-            q_raw = loads.tile([P, UNIT_TILES, D], BF16, tag="q_raw", bufs=UNITS)
-            nc.sync.dma_start(
-                out=q_raw[:],
-                in_=q[batch].rearrange("(p t) d -> p t d", t=ROWS_PER_PARTITION)[:, tiles, :],
-            )
-            q_raws.append(q_raw)
-            if half == 0:
-                ctx_raw = loads.tile([P, PACK, D], BF16, tag="ctx_raw", bufs=B)
+        for batch in range(B):
+            for part in range(LOADS_PER_BATCH):
+                tiles = slice(part * LOAD_TILES, (part + 1) * LOAD_TILES)
+                a_raw = loads.tile([P, LOAD_TILES, K], BF16, tag="a_raw", bufs=B * LOADS_PER_BATCH)
                 nc.sync.dma_start(
-                    out=ctx_raw[:].rearrange("p (u e) d -> p u (e d)", u=2),
-                    in_=context[batch].rearrange("(u p e) d -> p u (e d)", u=2, e=2),
+                    out=a_raw[:],
+                    in_=attn_weights[batch].rearrange("(p t) k -> p t k", t=BATCH_TILES)[:, tiles, :],
                 )
-                ctx_raws.append(ctx_raw)
+                a_raws.append(a_raw)
+                q_raw = loads.tile([P, LOAD_TILES, D], BF16, tag="q_raw", bufs=B * LOADS_PER_BATCH)
+                nc.sync.dma_start(
+                    out=q_raw[:],
+                    in_=q[batch].rearrange("(p t) d -> p t d", t=BATCH_TILES)[:, tiles, :],
+                )
+                q_raws.append(q_raw)
+                if part == 0:
+                    ctx_raw = loads.tile([P, PACK, D], BF16, tag="ctx_raw", bufs=B)
+                    nc.sync.dma_start(
+                        out=ctx_raw[:].rearrange("p (u e) d -> p u (e d)", u=2),
+                        in_=context[batch].rearrange("(u p e) d -> p u (e d)", u=2, e=2),
+                    )
+                    ctx_raws.append(ctx_raw)
 
         warm = const.tile([P, 1], F32)
         nc.vector.memset(warm[:], 0.0)
@@ -98,54 +99,30 @@ def tile_attention_pb_t_kernel(tc, attn_weights, context, q, W_out, b_out, out):
         out_acc, result = {}, {}
 
         def transpose_unit(unit):
-            a_words = a_raws[unit][:].bitcast(F32)
-            q_words = q_raws[unit][:].bitcast(F32)
-            for bank in range(UNIT_BANKS):
-                words_t = psum.tile([P, 2, BANK_ROWS], F32, tag="a_t")
-                for i in range(BANK_TILES):
-                    for u in range(2):
-                        nc.tensor.transpose(
-                            words_t[:, u, i * P : (i + 1) * P],
-                            a_words[:, bank * BANK_TILES + i, u * P : (u + 1) * P],
-                            ident[:],
-                        )
-                a_t[unit, bank] = words_t
+            load, part = divmod(unit, LOAD_UNITS)
+            a_words = a_raws[load][:].bitcast(F32)
+            q_words = q_raws[load][:].bitcast(F32)
+            a_words_t = psum.tile([P, 2, UNIT_ROWS], F32, tag="a_t")
             q_words_t = psum.tile([P, UNIT_ROWS], F32, tag="q_t")
-            for j in range(UNIT_TILES):
-                nc.tensor.transpose(q_words_t[:, j * P : (j + 1) * P], q_words[:, j, :], ident[:])
-            q_t[unit] = q_words_t
+            for i in range(UNIT_TILES):
+                j = part * UNIT_TILES + i
+                for u in range(2):
+                    nc.tensor.transpose(a_words_t[:, u, i * P : (i + 1) * P], a_words[:, j, u * P : (u + 1) * P], ident[:])
+                nc.tensor.transpose(q_words_t[:, i * P : (i + 1) * P], q_words[:, j, :], ident[:])
+            a_t[unit], q_t[unit] = a_words_t, q_words_t
 
         def copy_a_out(unit):
             grouped = work.tile([P, UNIT_ROWS, PACK], BF16, tag="a_grouped", align_bytes=64)
-            for bank in range(UNIT_BANKS):
-                nc.scalar.copy(
-                    out=grouped[:, bank * BANK_ROWS : (bank + 1) * BANK_ROWS, :].bitcast(F32),
-                    in_=a_t[unit, bank][:].rearrange("p u r -> p r u"),
-                )
+            nc.scalar.copy(out=grouped[:].bitcast(F32), in_=a_t[unit][:].rearrange("p u r -> p r u"))
             a_grouped[unit] = grouped
 
         def copy_q_out(unit):
-            both = work.tile([P, UNIT_ROWS, PACK], BF16, tag="comb", bufs=5, align_bytes=64)
+            both = work.tile([P, UNIT_ROWS, PACK], BF16, tag="comb", bufs=6, align_bytes=64)
             nc.vector.tensor_copy(
                 out=both[:].bitcast(F32),
                 in_=q_t[unit][:].unsqueeze(2).to_broadcast([P, UNIT_ROWS, 2]),
             )
             comb[unit] = both
-
-        def regroup_context(batch):
-            grouped = work.tile([P, 2, P, PACK], BF16, tag="ctx_grouped", bufs=2, align_bytes=64)
-            nc.vector.tensor_copy(out=grouped[:], in_=ctx_raws[batch][:].rearrange("p t (m f) -> p f m t", f=2))
-            ctx_grouped[batch] = grouped
-
-        def quantise_context(batch):
-            codes = work.tile([P, D], U32, tag="ctx_codes", align_bytes=64)
-            scales = work.tile([P, D], U8, tag="ctx_scales", align_bytes=64)
-            nc.vector.quantize_mx(
-                out=codes[:].bitcast(FP8X4),
-                scales=scales[:],
-                in_=ctx_grouped[batch][:].rearrange("p f m t -> p (f m t)"),
-            )
-            ctx_codes[batch], ctx_scales[batch] = codes, scales
 
         def quantise_a(unit):
             codes = work.tile([P, UNIT_ROWS], U32, tag="a_codes", align_bytes=64)
@@ -157,30 +134,39 @@ def tile_attention_pb_t_kernel(tc, attn_weights, context, q, W_out, b_out, out):
             )
             a_codes[unit], a_scales[unit] = codes, scales
 
+        def regroup_context(batch):
+            grouped = work.tile([P, 2, P, PACK], BF16, tag="ctx_grouped", bufs=2, align_bytes=64)
+            nc.vector.tensor_copy(out=grouped[:], in_=ctx_raws[batch][:].rearrange("p t (m f) -> p f m t", f=2))
+            ctx_grouped[batch] = grouped
+
+        def quantise_context(batch):
+            codes = work.tile([P, D], U32, tag="ctx_codes", bufs=3, align_bytes=64)
+            scales = work.tile([P, D], U8, tag="ctx_scales", bufs=3, align_bytes=64)
+            nc.vector.quantize_mx(
+                out=codes[:].bitcast(FP8X4),
+                scales=scales[:],
+                in_=ctx_grouped[batch][:].rearrange("p f m t -> p (f m t)"),
+            )
+            ctx_codes[batch], ctx_scales[batch] = codes, scales
+
         def multiply_mix(unit):
             batch = unit // UNITS_PER_BATCH
-            for bank in range(UNIT_BANKS):
-                rows = slice(bank * BANK_ROWS, (bank + 1) * BANK_ROWS)
-                acc = psum.tile([P, 2, BANK_ROWS], F32, tag="mix_t")
-                for f in range(2):
-                    feats = slice(f * P, (f + 1) * P)
-                    nc.tensor.matmul_mx(
-                        out=acc[:, f, :],
-                        lhsT=ctx_codes[batch][:, feats].bitcast(FP8X4),
-                        lhsT_scale=ctx_scales[batch][:, feats],
-                        rhs=a_codes[unit][:, rows].bitcast(FP8X4),
-                        rhs_scale=a_scales[unit][:, rows],
-                        start=True,
-                        stop=True,
-                    )
-                mix_t[unit, bank] = acc
+            acc = psum.tile([P, 2, UNIT_ROWS], F32, tag="mix_t")
+            for f in range(2):
+                feats = slice(f * P, (f + 1) * P)
+                nc.tensor.matmul_mx(
+                    out=acc[:, f, :],
+                    lhsT=ctx_codes[batch][:, feats].bitcast(FP8X4),
+                    lhsT_scale=ctx_scales[batch][:, feats],
+                    rhs=a_codes[unit][:].bitcast(FP8X4),
+                    rhs_scale=a_scales[unit][:],
+                    start=True,
+                    stop=True,
+                )
+            mix_t[unit] = acc
 
         def copy_mix_out(unit):
-            for bank in range(UNIT_BANKS):
-                nc.scalar.copy(
-                    out=comb[unit][:, bank * BANK_ROWS : (bank + 1) * BANK_ROWS, 0:2],
-                    in_=mix_t[unit, bank][:].rearrange("p f r -> p r f"),
-                )
+            nc.scalar.copy(out=comb[unit][:, :, 0:2], in_=mix_t[unit][:].rearrange("p f r -> p r f"))
 
         def quantise_comb(unit):
             codes = work.tile([P, UNIT_ROWS], U32, tag="comb_codes", align_bytes=64)
@@ -193,38 +179,36 @@ def tile_attention_pb_t_kernel(tc, attn_weights, context, q, W_out, b_out, out):
             comb_codes[unit], comb_scales[unit] = codes, scales
 
         def multiply_out(unit):
-            for bank in range(UNIT_BANKS):
-                acc = psum.tile([P, BANK_TILES, D], F32, tag="out_acc")
-                for i in range(BANK_TILES):
-                    j = bank * BANK_TILES + i
-                    nc.tensor.matmul_mx(
-                        out=acc[:, i, :],
-                        lhsT=comb_codes[unit][:, j * P : (j + 1) * P].bitcast(FP8X4),
-                        lhsT_scale=comb_scales[unit][:, j * P : (j + 1) * P],
-                        rhs=w_codes[:].bitcast(FP8X4),
-                        rhs_scale=w_scales[:],
-                        start=True,
-                        stop=True,
-                    )
-                out_acc[unit, bank] = acc
+            acc = psum.tile([P, UNIT_TILES, D], F32, tag="out_acc")
+            for i in range(UNIT_TILES):
+                rows = slice(i * P, (i + 1) * P)
+                nc.tensor.matmul_mx(
+                    out=acc[:, i, :],
+                    lhsT=comb_codes[unit][:, rows].bitcast(FP8X4),
+                    lhsT_scale=comb_scales[unit][:, rows],
+                    rhs=w_codes[:].bitcast(FP8X4),
+                    rhs_scale=w_scales[:],
+                    start=True,
+                    stop=True,
+                )
+            out_acc[unit] = acc
 
         def add_bias(unit):
-            summed = work.tile([P, UNIT_TILES, D], F32, tag="result", bufs=6)
-            for bank in range(UNIT_BANKS):
-                nc.vector.tensor_tensor(
-                    out=summed[:, bank * BANK_TILES : (bank + 1) * BANK_TILES, :],
-                    in0=out_acc[unit, bank][:],
-                    in1=bias[:].unsqueeze(1).to_broadcast([P, BANK_TILES, D]),
-                    op=ADD,
-                )
+            summed = work.tile([P, UNIT_TILES, D], F32, tag="result", bufs=8)
+            nc.vector.tensor_tensor(
+                out=summed[:],
+                in0=out_acc[unit][:],
+                in1=bias[:].unsqueeze(1).to_broadcast([P, UNIT_TILES, D]),
+                op=ADD,
+            )
             result[unit] = summed
 
         def tanh_and_store(unit):
-            batch, half = divmod(unit, UNITS_PER_BATCH)
-            tiles = slice(half * UNIT_TILES, (half + 1) * UNIT_TILES)
+            batch, part = divmod(unit, UNITS_PER_BATCH)
+            tiles = slice(part * UNIT_TILES, (part + 1) * UNIT_TILES)
             nc.scalar.activation(out=result[unit][:], in_=result[unit][:], func=TANH)
             nc.sync.dma_start(
-                out=out[batch].rearrange("(p t) o -> p t o", t=ROWS_PER_PARTITION)[:, tiles, :],
+                out=out[batch].rearrange("(p t) o -> p t o", t=BATCH_TILES)[:, tiles, :],
                 in_=result[unit][:],
             )
 
@@ -232,11 +216,11 @@ def tile_attention_pb_t_kernel(tc, attn_weights, context, q, W_out, b_out, out):
             if 0 <= unit < UNITS:
                 stage(unit)
 
-        def run_for_batch(stage, step):
-            if step % UNITS_PER_BATCH == 0 and step < UNITS:
-                stage(step // UNITS_PER_BATCH)
+        def run_for_batch(stage, unit):
+            if unit % UNITS_PER_BATCH == 0:
+                run(lambda first_unit: stage(first_unit // UNITS_PER_BATCH), unit)
 
-        for step in range(UNITS + LAG_OUT):
+        for step in range(UNITS + LAG_TANH):
             run(transpose_unit, step)
             run(multiply_mix, step - LAG_MIX)
             run(multiply_out, step - LAG_OUT)
@@ -247,5 +231,5 @@ def tile_attention_pb_t_kernel(tc, attn_weights, context, q, W_out, b_out, out):
             run(quantise_a, step - LAG_QUANTISE_A)
             run(copy_mix_out, step - LAG_MIX)
             run(quantise_comb, step - LAG_QUANTISE_COMB)
-            run_for_batch(quantise_context, step)
-            run(tanh_and_store, step - LAG_OUT)
+            run_for_batch(quantise_context, step - 1)
+            run(tanh_and_store, step - LAG_TANH)

@@ -28,9 +28,11 @@ LOADS_PER_BATCH = BATCH_TILES // LOAD_TILES
 
 LAG_QUANTISE_A = 1
 LAG_MIX = 3
-LAG_QUANTISE_COMB = 4
-LAG_OUT = 6
-LAG_TANH = 7
+LAG_JOIN = 4
+LAG_QUANTISE_COMB = 5
+LAG_OUT = 7
+LAG_TANH = 8
+W_STEP = 5
 
 
 def tile_attention_pb_t_kernel(tc, attn_weights, context, q, W_out, b_out, out):
@@ -42,26 +44,26 @@ def tile_attention_pb_t_kernel(tc, attn_weights, context, q, W_out, b_out, out):
         work = stack.enter_context(tc.tile_pool(name="work", bufs=4))
         psum = stack.enter_context(tc.psum_pool(name="psum", bufs=2))
 
-        w_raw = const.tile([P, D // P, C], BF16)
-        nc.scalar.dma_start(out=w_raw[:], in_=W_out.rearrange("(j p) c -> p j c", p=P))
-        bias_bf16 = const.tile([P, D], BF16)
-        nc.scalar.dma_start(out=bias_bf16[:], in_=b_out.partition_broadcast(P))
-
         a_raws, q_raws, ctx_raws = [], [], []
+        w_raw = const.tile([P, D // P, C], BF16)
+        bias_bf16 = const.tile([P, D], BF16)
         for batch in range(B):
+            a_rows = attn_weights[batch].rearrange("(p t) k -> p t k", t=BATCH_TILES)
+            q_rows = q[batch].rearrange("(p t) d -> p t d", t=BATCH_TILES)
             for part in range(LOADS_PER_BATCH):
-                tiles = slice(part * LOAD_TILES, (part + 1) * LOAD_TILES)
+                first = part * LOAD_TILES
                 a_raw = loads.tile([P, LOAD_TILES, K], BF16, tag="a_raw", bufs=B * LOADS_PER_BATCH)
-                nc.sync.dma_start(
-                    out=a_raw[:],
-                    in_=attn_weights[batch].rearrange("(p t) k -> p t k", t=BATCH_TILES)[:, tiles, :],
-                )
+                cuts = LOAD_UNITS if (batch, part) == (0, 0) else 1
+                width = LOAD_TILES // cuts
+                for cut in range(cuts):
+                    nc.sync.dma_start(
+                        out=a_raw[:, cut * width : (cut + 1) * width, :],
+                        in_=a_rows[:, first + cut * width : first + (cut + 1) * width, :],
+                    )
+                    if cut == 0:
+                        q_raw = loads.tile([P, LOAD_TILES, D], BF16, tag="q_raw", bufs=B * LOADS_PER_BATCH)
+                        nc.sync.dma_start(out=q_raw[:], in_=q_rows[:, first : first + LOAD_TILES, :])
                 a_raws.append(a_raw)
-                q_raw = loads.tile([P, LOAD_TILES, D], BF16, tag="q_raw", bufs=B * LOADS_PER_BATCH)
-                nc.sync.dma_start(
-                    out=q_raw[:],
-                    in_=q[batch].rearrange("(p t) d -> p t d", t=BATCH_TILES)[:, tiles, :],
-                )
                 q_raws.append(q_raw)
                 if part == 0:
                     ctx_raw = loads.tile([P, PACK, D], BF16, tag="ctx_raw", bufs=B)
@@ -70,6 +72,9 @@ def tile_attention_pb_t_kernel(tc, attn_weights, context, q, W_out, b_out, out):
                         in_=context[batch].rearrange("(u p e) d -> p u (e d)", u=2, e=2),
                     )
                     ctx_raws.append(ctx_raw)
+            if batch == 0:
+                nc.sync.dma_start(out=w_raw[:], in_=W_out.rearrange("(j p) c -> p j c", p=P))
+                nc.sync.dma_start(out=bias_bf16[:], in_=b_out.partition_broadcast(P))
 
         warm = const.tile([P, 1], F32)
         nc.vector.memset(warm[:], 0.0)
@@ -78,24 +83,26 @@ def tile_attention_pb_t_kernel(tc, attn_weights, context, q, W_out, b_out, out):
         ident = const.tile([P, P], F32)
         make_identity(nc, ident[:])
 
-        w_words = w_raw[:].bitcast(F32)
-        w_t = psum.tile([P, 2, D], F32, tag="a_t")
-        for j in range(D // P):
-            for u in range(2):
-                nc.tensor.transpose(w_t[:, u, j * P : (j + 1) * P], w_words[:, j, u * P : (u + 1) * P], ident[:])
         w_grouped = const.tile([P, D, PACK], BF16, align_bytes=64)
-        nc.vector.tensor_copy(out=w_grouped[:].bitcast(F32), in_=w_t[:].rearrange("p u o -> p o u"))
-        bias = const.tile([P, D], F32)
-        nc.vector.tensor_copy(out=bias[:], in_=bias_bf16[:])
         w_codes = const.tile([P, D], U32, align_bytes=64)
         w_scales = const.tile([P, D], U8, align_bytes=64)
-        nc.vector.quantize_mx(
-            out=w_codes[:].bitcast(FP8X4), scales=w_scales[:], in_=w_grouped[:].rearrange("p o t -> p (o t)")
-        )
+        bias = const.tile([P, D], F32)
+
+        def prepare_w():
+            w_words = w_raw[:].bitcast(F32)
+            w_t = psum.tile([P, 2, D], F32, tag="a_t")
+            for j in range(D // P):
+                for u in range(2):
+                    nc.tensor.transpose(w_t[:, u, j * P : (j + 1) * P], w_words[:, j, u * P : (u + 1) * P], ident[:])
+            nc.vector.tensor_copy(out=w_grouped[:].bitcast(F32), in_=w_t[:].rearrange("p u o -> p o u"))
+            nc.vector.tensor_copy(out=bias[:], in_=bias_bf16[:])
+            nc.vector.quantize_mx(
+                out=w_codes[:].bitcast(FP8X4), scales=w_scales[:], in_=w_grouped[:].rearrange("p o t -> p (o t)")
+            )
 
         a_t, q_t, a_grouped, a_codes, a_scales = {}, {}, {}, {}, {}
         ctx_grouped, ctx_codes, ctx_scales = {}, {}, {}
-        mix_t, comb, comb_codes, comb_scales = {}, {}, {}, {}
+        mix_t, halves, comb, comb_codes, comb_scales = {}, {}, {}, {}, {}
         out_acc, result = {}, {}
 
         def transpose_unit(unit):
@@ -117,12 +124,12 @@ def tile_attention_pb_t_kernel(tc, attn_weights, context, q, W_out, b_out, out):
             a_grouped[unit] = grouped
 
         def copy_q_out(unit):
-            both = work.tile([P, UNIT_ROWS, PACK], BF16, tag="comb", bufs=6, align_bytes=64)
-            nc.vector.tensor_copy(
-                out=both[:].bitcast(F32),
-                in_=q_t[unit][:].unsqueeze(2).to_broadcast([P, UNIT_ROWS, 2]),
-            )
-            comb[unit] = both
+            planes = work.tile([P, 2, UNIT_ROWS, 2], BF16, tag="halves", bufs=6)
+            if unit % 2 == 0:
+                nc.scalar.copy(out=planes[:, 1, :, :].bitcast(F32), in_=q_t[unit][:].unsqueeze(2))
+            else:
+                nc.vector.tensor_copy(out=planes[:, 1, :, :].bitcast(F32), in_=q_t[unit][:].unsqueeze(2))
+            halves[unit] = planes
 
         def quantise_a(unit):
             codes = work.tile([P, UNIT_ROWS], U32, tag="a_codes", align_bytes=64)
@@ -166,7 +173,15 @@ def tile_attention_pb_t_kernel(tc, attn_weights, context, q, W_out, b_out, out):
             mix_t[unit] = acc
 
         def copy_mix_out(unit):
-            nc.scalar.copy(out=comb[unit][:, :, 0:2], in_=mix_t[unit][:].rearrange("p f r -> p r f"))
+            nc.scalar.copy(out=halves[unit][:, 0, :, :], in_=mix_t[unit][:].rearrange("p f r -> p r f"))
+
+        def join_halves(unit):
+            both = work.tile([P, UNIT_ROWS, PACK], BF16, tag="comb", align_bytes=64)
+            nc.vector.tensor_copy(
+                out=both[:].bitcast(F32),
+                in_=halves[unit][:].bitcast(F32).rearrange("p u r o -> p r (u o)"),
+            )
+            comb[unit] = both
 
         def quantise_comb(unit):
             codes = work.tile([P, UNIT_ROWS], U32, tag="comb_codes", align_bytes=64)
@@ -221,6 +236,8 @@ def tile_attention_pb_t_kernel(tc, attn_weights, context, q, W_out, b_out, out):
                 run(lambda first_unit: stage(first_unit // UNITS_PER_BATCH), unit)
 
         for step in range(UNITS + LAG_TANH):
+            if step == W_STEP:
+                prepare_w()
             run(transpose_unit, step)
             run(multiply_mix, step - LAG_MIX)
             run(multiply_out, step - LAG_OUT)
@@ -230,6 +247,7 @@ def tile_attention_pb_t_kernel(tc, attn_weights, context, q, W_out, b_out, out):
             run_for_batch(regroup_context, step)
             run(quantise_a, step - LAG_QUANTISE_A)
             run(copy_mix_out, step - LAG_MIX)
+            run(join_halves, step - LAG_JOIN)
             run(quantise_comb, step - LAG_QUANTISE_COMB)
             run_for_batch(quantise_context, step - 1)
             run(tanh_and_store, step - LAG_TANH)

from contextlib import ExitStack

import concourse.mybir as mybir
from concourse.masks import make_identity

BF16 = mybir.dt.bfloat16
F32 = mybir.dt.float32
U32 = mybir.dt.uint32
U8 = mybir.dt.uint8
FP8X4 = mybir.dt.float8_e4m3fn_x4
TANH = mybir.ActivationFunctionType.Tanh
ADD = mybir.AluOpType.add

B, Q, K, D = 8, 1024, 512, 256
C = D + D
FLOPS = 2 * B * Q * K * D + 2 * B * Q * C * D

P = 128
PACK = 4
BATCH_TILES = Q // P
UNIT_TILES = 2
UNIT_ROWS = UNIT_TILES * P
UNITS_PER_BATCH = BATCH_TILES // UNIT_TILES
UNITS = B * UNITS_PER_BATCH
LOAD_UNITS = 2
LOAD_TILES = LOAD_UNITS * UNIT_TILES
LOADS_PER_BATCH = BATCH_TILES // LOAD_TILES

LAG_QUANTISE_A = 1
LAG_MIX = 3
LAG_JOIN = 4
LAG_QUANTISE_COMB = 5
LAG_OUT = 7
LAG_TANH = 8
W_STEP = 5


def tile_attention_pb_t_kernel(tc, attn_weights, context, q, W_out, b_out, out):
    nc = tc.nc
    with ExitStack() as stack:
        stack.enter_context(tc.manual_schedule())
        const = stack.enter_context(tc.tile_pool(name="const", bufs=1))
        loads = stack.enter_context(tc.tile_pool(name="loads", bufs=1))
        work = stack.enter_context(tc.tile_pool(name="work", bufs=4))
        psum = stack.enter_context(tc.psum_pool(name="psum", bufs=2))

        a_raws, q_raws, ctx_raws = [], [], []
        w_raw = const.tile([P, D // P, C], BF16)
        bias_bf16 = const.tile([P, D], BF16)
        for batch in range(B):
            a_rows = attn_weights[batch].rearrange("(p t) k -> p t k", t=BATCH_TILES)
            q_rows = q[batch].rearrange("(p t) d -> p t d", t=BATCH_TILES)
            for part in range(LOADS_PER_BATCH):
                first = part * LOAD_TILES
                a_raw = loads.tile([P, LOAD_TILES, K], BF16, tag="a_raw", bufs=B * LOADS_PER_BATCH)
                cuts = LOAD_UNITS if (batch, part) == (0, 0) else 1
                width = LOAD_TILES // cuts
                for cut in range(cuts):
                    nc.sync.dma_start(
                        out=a_raw[:, cut * width : (cut + 1) * width, :],
                        in_=a_rows[:, first + cut * width : first + (cut + 1) * width, :],
                    )
                    if cut == 0:
                        q_raw = loads.tile([P, LOAD_TILES, D], BF16, tag="q_raw", bufs=B * LOADS_PER_BATCH)
                        nc.sync.dma_start(out=q_raw[:], in_=q_rows[:, first : first + LOAD_TILES, :])
                a_raws.append(a_raw)
                q_raws.append(q_raw)
                if part == 0:
                    ctx_raw = loads.tile([P, PACK, D], BF16, tag="ctx_raw", bufs=B)
                    nc.sync.dma_start(
                        out=ctx_raw[:].rearrange("p (u e) d -> p u (e d)", u=2),
                        in_=context[batch].rearrange("(u p e) d -> p u (e d)", u=2, e=2),
                    )
                    ctx_raws.append(ctx_raw)
            if batch == 0:
                nc.sync.dma_start(out=w_raw[:], in_=W_out.rearrange("(j p) c -> p j c", p=P))
                nc.sync.dma_start(out=bias_bf16[:], in_=b_out.partition_broadcast(P))

        warm = const.tile([P, 1], F32)
        nc.vector.memset(warm[:], 0.0)
        nc.scalar.activation(out=warm[:], in_=warm[:], func=TANH)

        ident = const.tile([P, P], F32)
        make_identity(nc, ident[:])

        w_grouped = const.tile([P, D, PACK], BF16, align_bytes=64)
        w_codes = const.tile([P, D], U32, align_bytes=64)
        w_scales = const.tile([P, D], U8, align_bytes=64)
        bias = const.tile([P, D], F32)

        def prepare_w():
            w_words = w_raw[:].bitcast(F32)
            w_t = psum.tile([P, 2, D], F32, tag="a_t")
            for j in range(D // P):
                for u in range(2):
                    nc.tensor.transpose(w_t[:, u, j * P : (j + 1) * P], w_words[:, j, u * P : (u + 1) * P], ident[:])
            nc.vector.tensor_copy(out=w_grouped[:].bitcast(F32), in_=w_t[:].rearrange("p u o -> p o u"))
            nc.vector.tensor_copy(out=bias[:], in_=bias_bf16[:])
            nc.vector.quantize_mx(
                out=w_codes[:].bitcast(FP8X4), scales=w_scales[:], in_=w_grouped[:].rearrange("p o t -> p (o t)")
            )

        a_t, q_t, a_grouped, a_codes, a_scales = {}, {}, {}, {}, {}
        ctx_grouped, ctx_codes, ctx_scales = {}, {}, {}
        mix_t, halves, comb, comb_codes, comb_scales = {}, {}, {}, {}, {}
        out_acc, result = {}, {}

        def transpose_unit(unit):
            load, part = divmod(unit, LOAD_UNITS)
            a_words = a_raws[load][:].bitcast(F32)
            q_words = q_raws[load][:].bitcast(F32)
            a_words_t = psum.tile([P, 2, UNIT_ROWS], F32, tag="a_t")
            q_words_t = psum.tile([P, UNIT_ROWS], F32, tag="q_t")
            for i in range(UNIT_TILES):
                j = part * UNIT_TILES + i
                for u in range(2):
                    nc.tensor.transpose(a_words_t[:, u, i * P : (i + 1) * P], a_words[:, j, u * P : (u + 1) * P], ident[:])
                nc.tensor.transpose(q_words_t[:, i * P : (i + 1) * P], q_words[:, j, :], ident[:])
            a_t[unit], q_t[unit] = a_words_t, q_words_t

        def copy_a_out(unit):
            grouped = work.tile([P, UNIT_ROWS, PACK], BF16, tag="a_grouped", align_bytes=64)
            nc.scalar.copy(out=grouped[:].bitcast(F32), in_=a_t[unit][:].rearrange("p u r -> p r u"))
            a_grouped[unit] = grouped

        def copy_q_out(unit):
            planes = work.tile([P, 2, UNIT_ROWS, 2], BF16, tag="halves", bufs=6)
            if unit % 2 == 0:
                nc.scalar.copy(out=planes[:, 1, :, :].bitcast(F32), in_=q_t[unit][:].unsqueeze(2))
            else:
                nc.vector.tensor_copy(out=planes[:, 1, :, :].bitcast(F32), in_=q_t[unit][:].unsqueeze(2))
            halves[unit] = planes

        def quantise_a(unit):
            codes = work.tile([P, UNIT_ROWS], U32, tag="a_codes", align_bytes=64)
            scales = work.tile([P, UNIT_ROWS], U8, tag="a_scales", align_bytes=64)
            nc.vector.quantize_mx(
                out=codes[:].bitcast(FP8X4),
                scales=scales[:],
                in_=a_grouped[unit][:].rearrange("p r t -> p (r t)"),
            )
            a_codes[unit], a_scales[unit] = codes, scales

        def regroup_context(batch):
            grouped = work.tile([P, 2, P, PACK], BF16, tag="ctx_grouped", bufs=2, align_bytes=64)
            nc.vector.tensor_copy(out=grouped[:], in_=ctx_raws[batch][:].rearrange("p t (m f) -> p f m t", f=2))
            ctx_grouped[batch] = grouped

        def quantise_context(batch):
            codes = work.tile([P, D], U32, tag="ctx_codes", bufs=3, align_bytes=64)
            scales = work.tile([P, D], U8, tag="ctx_scales", bufs=3, align_bytes=64)
            nc.vector.quantize_mx(
                out=codes[:].bitcast(FP8X4),
                scales=scales[:],
                in_=ctx_grouped[batch][:].rearrange("p f m t -> p (f m t)"),
            )
            ctx_codes[batch], ctx_scales[batch] = codes, scales

        def multiply_mix(unit):
            batch = unit // UNITS_PER_BATCH
            acc = psum.tile([P, 2, UNIT_ROWS], F32, tag="mix_t")
            for f in range(2):
                feats = slice(f * P, (f + 1) * P)
                nc.tensor.matmul_mx(
                    out=acc[:, f, :],
                    lhsT=ctx_codes[batch][:, feats].bitcast(FP8X4),
                    lhsT_scale=ctx_scales[batch][:, feats],
                    rhs=a_codes[unit][:].bitcast(FP8X4),
                    rhs_scale=a_scales[unit][:],
                    start=True,
                    stop=True,
                )
            mix_t[unit] = acc

        def copy_mix_out(unit):
            nc.scalar.copy(out=halves[unit][:, 0, :, :], in_=mix_t[unit][:].rearrange("p f r -> p r f"))

        def join_halves(unit):
            both = work.tile([P, UNIT_ROWS, PACK], BF16, tag="comb", align_bytes=64)
            nc.vector.tensor_copy(
                out=both[:].bitcast(F32),
                in_=halves[unit][:].bitcast(F32).rearrange("p u r o -> p r (u o)"),
            )
            comb[unit] = both

        def quantise_comb(unit):
            codes = work.tile([P, UNIT_ROWS], U32, tag="comb_codes", align_bytes=64)
            scales = work.tile([P, UNIT_ROWS], U8, tag="comb_scales", align_bytes=64)
            nc.vector.quantize_mx(
                out=codes[:].bitcast(FP8X4),
                scales=scales[:],
                in_=comb[unit][:].rearrange("p r t -> p (r t)"),
            )
            comb_codes[unit], comb_scales[unit] = codes, scales

        def multiply_out(unit):
            acc = psum.tile([P, UNIT_TILES, D], F32, tag="out_acc")
            for i in range(UNIT_TILES):
                rows = slice(i * P, (i + 1) * P)
                nc.tensor.matmul_mx(
                    out=acc[:, i, :],
                    lhsT=comb_codes[unit][:, rows].bitcast(FP8X4),
                    lhsT_scale=comb_scales[unit][:, rows],
                    rhs=w_codes[:].bitcast(FP8X4),
                    rhs_scale=w_scales[:],
                    start=True,
                    stop=True,
                )
            out_acc[unit] = acc

        def add_bias(unit):
            summed = work.tile([P, UNIT_TILES, D], F32, tag="result", bufs=8)
            nc.vector.tensor_tensor(
                out=summed[:],
                in0=out_acc[unit][:],
                in1=bias[:].unsqueeze(1).to_broadcast([P, UNIT_TILES, D]),
                op=ADD,
            )
            result[unit] = summed

        def tanh_and_store(unit):
            batch, part = divmod(unit, UNITS_PER_BATCH)
            tiles = slice(part * UNIT_TILES, (part + 1) * UNIT_TILES)
            nc.scalar.activation(out=result[unit][:], in_=result[unit][:], func=TANH)
            nc.sync.dma_start(
                out=out[batch].rearrange("(p t) o -> p t o", t=BATCH_TILES)[:, tiles, :],
                in_=result[unit][:],
            )

        def run(stage, unit):
            if 0 <= unit < UNITS:
                stage(unit)

        def run_for_batch(stage, unit):
            if unit % UNITS_PER_BATCH == 0:
                run(lambda first_unit: stage(first_unit // UNITS_PER_BATCH), unit)

        for step in range(UNITS + LAG_TANH):
            if step == W_STEP:
                prepare_w()
            run(transpose_unit, step)
            run(multiply_mix, step - LAG_MIX)
            run(multiply_out, step - LAG_OUT)
            run(copy_a_out, step)
            run(copy_q_out, step)
            run(add_bias, step - LAG_OUT)
            run_for_batch(regroup_context, step)
            run(quantise_a, step - LAG_QUANTISE_A)
            run(copy_mix_out, step - LAG_MIX)
            run(join_halves, step - LAG_JOIN)
            run(quantise_comb, step - LAG_QUANTISE_COMB)
            run_for_batch(quantise_context, step - 1)
            run(tanh_and_store, step - LAG_TANH)
